import numpy as np
import ml_dtypes


def mxq(x, axis, fmt="e4m3"):
    dtype, down = {"e4m3": (ml_dtypes.float8_e4m3fn, 7), "e5m2": (ml_dtypes.float8_e5m2, 14)}[fmt]
    v = np.moveaxis(np.asarray(x, np.float32).astype(ml_dtypes.bfloat16).astype(np.float64), axis, -1)
    blocks = v.reshape(v.shape[:-1] + (-1, 32))
    amax = np.abs(blocks).max(-1, keepdims=True)
    byte = np.maximum(np.where(amax > 0, np.frexp(amax)[1] - 1 + 127, 0) - down, 1)
    scale = np.exp2(byte - 127.0)
    codes = (blocks / scale).astype(np.float32).astype(dtype).astype(np.float64)
    return np.moveaxis((codes * scale).reshape(v.shape), -1, axis)


WIDE = False


def mx_kscale(k):
    if not WIDE:
        return np.ones(k)
    levels = np.array([10, -10, 5, -5, 0])
    a = np.random.permutation(np.resize(levels, k // 512 * 4)).reshape(k // 512, 4)
    idx = np.arange(k)
    return np.exp2(a[idx // 512, idx % 128 // 32])


BF16 = ml_dtypes.bfloat16


def bf(x):
    return np.asarray(x, np.float32).astype(BF16)


def f64(x):
    return np.asarray(x).astype(np.float64)


E2M1 = np.array([0.0, 0.5, 1.0, 1.5, 2.0, 3.0, 4.0, 6.0, -0.0, -0.5, -1.0, -1.5, -2.0, -3.0, -4.0, -6.0])


def pack_weight(w, fmt):
    k, n = w.shape
    w = f64(bf(w)).reshape(k // 32, 32, n)
    amax = np.abs(w).max(1)
    if fmt == "e4m3":
        byte = np.frexp(amax)[1] - 1 + 127 - 7
    else:
        mant, ex = np.frexp(amax / 6.0)
        byte = np.where(mant > 0.5, ex, ex - 1) + 127
    byte = np.clip(np.where(amax > 0, byte, 1), 1, 254)
    scaled = (w * np.exp2(127.0 - byte)[:, None, :]).reshape(k, n).astype(np.float32)
    by_word = np.ascontiguousarray(scaled.reshape(k // 512, 128, 4, n).transpose(0, 1, 3, 2))
    if fmt == "e4m3":
        words = by_word.astype(ml_dtypes.float8_e4m3fn).view(np.uint8)
    else:
        c = by_word.astype(ml_dtypes.float4_e2m1fn).view(np.uint8) & 0xF
        words = c[..., 0::2] | (c[..., 1::2] << 4)
    return np.ascontiguousarray(words), np.ascontiguousarray(byte.astype(np.uint8).reshape(k // 512, 16, n))


def unpack_weight(words, scales, fmt):
    g, p, n, _ = words.shape
    if fmt == "e4m3":
        vals = np.ascontiguousarray(words).view(ml_dtypes.float8_e4m3fn).astype(np.float64)
    else:
        nib = np.empty((g, p, n, 4), np.uint8)
        nib[..., 0::2] = words & 0xF
        nib[..., 1::2] = words >> 4
        vals = E2M1[nib]
    vals = vals * np.repeat(np.exp2(scales.astype(np.float64) - 127.0), 8, axis=1)[..., None]
    return vals.transpose(0, 1, 3, 2).reshape(g * 512, n)


B, S, DIM, H, DH, DV, R = 2, 2048, 512, 4, 128, 128, 512
EPS = 1e-6
N = H * (DH + DV)
FMT = "e4m3"


def rmsnorm(c, w):
    norm = np.mean(c * c, axis=-1, keepdims=True)
    return w * (c * (1.0 / np.sqrt(norm + EPS)))


def setup_inputs():
    s, t = mx_kscale(DIM), mx_kscale(R)
    x = bf(np.random.standard_normal((B, S, DIM)) * s)
    wa = np.random.standard_normal((R, DIM)) / np.sqrt(DIM) / s[None, :]
    wa_words, wa_scales = pack_weight(np.ascontiguousarray(wa.T), FMT)
    wkv_a_b = bf(np.random.standard_normal(R) * 0.3)
    kv_norm_w = bf((1.0 + 0.1 * np.random.standard_normal(R)) * t)
    wb = np.random.standard_normal((N, R)) / np.sqrt(R) / t[None, :]
    wb_words, wb_scales = pack_weight(np.ascontiguousarray(wb.T), FMT)
    wkv_b_b = bf(np.random.standard_normal(N) * 0.3)
    return {"x": x,
            "wkv_a_w_words": wa_words,
            "wkv_a_w_scales": wa_scales,
            "wkv_a_b": wkv_a_b,
            "kv_norm_w": kv_norm_w,
            "wkv_b_w_words": wb_words,
            "wkv_b_w_scales": wb_scales,
            "wkv_b_b": wkv_b_b}


def reference(x, wkv_a_w_words, wkv_a_w_scales, wkv_a_b, kv_norm_w, wkv_b_w_words, wkv_b_w_scales, wkv_b_b):
    c = (mxq(f64(x), 2, "e4m3") @ unpack_weight(wkv_a_w_words, wkv_a_w_scales, FMT)) + f64(wkv_a_b)
    kv_c = rmsnorm(c, f64(kv_norm_w))
    kv = (mxq(kv_c, 2, "e4m3") @ unpack_weight(wkv_b_w_words, wkv_b_w_scales, FMT)) + f64(wkv_b_b)
    kv = kv.reshape(B, S, H, DH + DV)
    return kv[..., :DH], kv[..., DH:]

@@ -1,0 +1,249 @@
+from contextlib import ExitStack
+
+import concourse.mybir as mybir
+from concourse.masks import make_identity
+
+F32 = mybir.dt.float32
+BF16 = mybir.dt.bfloat16
+I32 = mybir.dt.int32
+U32 = mybir.dt.uint32
+U8 = mybir.dt.uint8
+FP8X4 = mybir.dt.float8_e4m3fn_x4
+ADD = mybir.AluOpType.add
+MULT = mybir.AluOpType.mult
+ACT = mybir.ActivationFunctionType
+
+P = 128
+PACK = 4
+TOKENS = 2 * 2048
+DIM = 512
+RANK = 512
+HEADS = 4
+HEAD_DIM = 128
+KV = HEADS * 2 * HEAD_DIM
+BANK = 512
+EPS = 1e-6
+
+TILES = 2
+UNITS = TOKENS // (TILES * P)
+
+FLOPS = 2 * TOKENS * (DIM * RANK + RANK * KV)
+
+
+def tile_mla_pa_t_kernel(
+    tc,
+    x,
+    wkv_a_w_words,
+    wkv_a_w_scales,
+    wkv_a_b,
+    kv_norm_w,
+    wkv_b_w_words,
+    wkv_b_w_scales,
+    wkv_b_b,
+    out_0,
+    out_1,
+):
+    nc = tc.nc
+    x_units = x.flatten_outer_dims().rearrange("(u p i) d -> u p i d", p=P, i=TILES)
+    out_units = [
+        o.rearrange("b s h d -> (b s) (h d)").rearrange("(u p i) c -> u p (i c)", p=P, i=TILES)
+        for o in (out_0, out_1)
+    ]
+
+    with ExitStack() as ctx:
+        const = ctx.enter_context(tc.tile_pool(name="const", bufs=1))
+        work = ctx.enter_context(tc.tile_pool(name="work", bufs=2))
+        psum = ctx.enter_context(tc.psum_pool(name="psum", bufs=1))
+        ctx.enter_context(tc.manual_schedule())
+
+        planes = const.tile([P, RANK + KV], U8, align_bytes=64)
+        nc.vector.memset(planes[:].bitcast(I32), 0)
+        wa_plane = planes[:, 0:RANK]
+        wb_plane = planes[:, RANK : RANK + KV]
+        wa_words = const.tile([P, RANK], U32, align_bytes=64)
+        wb_words = const.tile([P, KV], U32, align_bytes=64)
+        x_all = const.tile([P, UNITS, TILES, DIM], BF16)
+
+        def load_weight(words, plane, dram_words, dram_scales):
+            for q in range(4):
+                nc.sync.dma_start(
+                    out=plane[32 * q : 32 * q + 4, :].bitcast(I32),
+                    in_=dram_scales[0, 4 * q : 4 * q + 4, :].bitcast(I32),
+                )
+            nc.sync.dma_start(
+                out=words[:].bitcast(I32),
+                in_=dram_words[0].rearrange("p n t -> p (n t)").bitcast(I32),
+            )
+
+        load_weight(wa_words, wa_plane, wkv_a_w_words, wkv_a_w_scales)
+        for u in range(2):
+            nc.sync.dma_start(out=x_all[:, u], in_=x_units[u])
+        load_weight(wb_words, wb_plane, wkv_b_w_words, wkv_b_w_scales)
+        for u in range(2, UNITS):
+            nc.sync.dma_start(out=x_all[:, u], in_=x_units[u])
+
+        b1_raw = const.tile([P, RANK], BF16)
+        gain_raw = const.tile([P, RANK], BF16)
+        b2_all = const.tile([P, KV], BF16)
+        nc.scalar.dma_start(out=b1_raw[:], in_=wkv_a_b.partition_broadcast(P))
+        nc.scalar.dma_start(out=gain_raw[:], in_=kv_norm_w.partition_broadcast(P))
+        nc.scalar.dma_start(out=b2_all[:], in_=wkv_b_b.partition_broadcast(P))
+        eps = const.tile([P, 1], F32)
+        nc.vector.memset(eps[:], EPS)
+        warm = const.tile([P, 1], F32)
+        nc.scalar.activation(out=warm[:], in_=eps[:], func=ACT.Sqrt)
+        b1_all = const.tile([P, PACK, P], F32)
+        gain_all = const.tile([P, PACK, P], F32)
+        nc.vector.tensor_copy(out=b1_all[:], in_=b1_raw[:].rearrange("p (m t) -> p t m", t=PACK))
+        nc.vector.tensor_copy(out=gain_all[:], in_=gain_raw[:].rearrange("p (m t) -> p t m", t=PACK))
+
+        ident_f32 = const.tile([P, P], F32)
+        make_identity(nc, ident_f32[:])
+        ident_bf16 = const.tile([P, P], BF16)
+        make_identity(nc, ident_bf16[:])
+
+        x_flipped, x_grouped, x_mx = {}, {}, {}
+        latent_ps, latent, gained, rms, inv_rms = {}, {}, {}, {}, {}
+        kvc_flipped, kvc_grouped, kvc_mx, kv_ps = {}, {}, {}, {}
+
+        def flip_x(u):
+            x_t = psum.tile([P, TILES, 2, P], F32)
+            for i in range(TILES):
+                words = x_all[:, u, i, :].bitcast(F32)
+                for h in range(2):
+                    nc.tensor.transpose(x_t[:, i, h, :], words[:, h : DIM // 2 : 2], ident_f32[:])
+            x_flipped[u] = x_t
+
+        def copy_x(u):
+            grouped = work.tile([P, TILES, P, PACK], BF16, align_bytes=64, name="x_grouped")
+            nc.scalar.copy(out=grouped[:].bitcast(F32), in_=x_flipped[u][:].rearrange("p i h r -> p i r h"))
+            x_grouped[u] = grouped
+
+        def quantise(grouped, name, bufs):
+            codes = work.tile([P, TILES * P], U32, align_bytes=64, name=name + "_codes", bufs=bufs)
+            plane = work.tile([P, TILES * P], U8, align_bytes=64, name=name + "_plane", bufs=bufs)
+            nc.vector.quantize_mx(
+                out=codes[:].bitcast(FP8X4),
+                scales=plane[:],
+                in_=grouped[:].rearrange("p i r t -> p (i r t)"),
+            )
+            return codes, plane
+
+        def multiply(out, mx, i, words, plane):
+            codes, scales = mx
+            tok = slice(i * P, (i + 1) * P)
+            nc.tensor.matmul_mx(
+                out=out,
+                lhsT=codes[:, tok].bitcast(FP8X4),
+                lhsT_scale=scales[:, tok],
+                rhs=words.bitcast(FP8X4),
+                rhs_scale=plane,
+                start=True,
+                stop=True,
+            )
+
+        def latent_matmul(u):
+            latent_ps[u] = []
+            for i in range(TILES):
+                c_ps = psum.tile([P, RANK], F32, bufs=TILES)
+                multiply(c_ps[:], x_mx[u], i, wa_words[:], wa_plane)
+                latent_ps[u].append(c_ps)
+
+        def latent_bias_and_gain(u):
+            latent[u], gained[u] = [], []
+            for i in range(TILES):
+                c_sb = work.tile([P, PACK, P], F32, bufs=2 * TILES)
+                nc.vector.tensor_tensor(
+                    out=c_sb[:],
+                    in0=latent_ps[u][i][:].rearrange("p (m t) -> p t m", t=PACK),
+                    in1=b1_all[:],
+                    op=ADD,
+                )
+                c_gain = work.tile([P, PACK, P], F32, bufs=3 * TILES)
+                nc.gpsimd.tensor_tensor(out=c_gain[:], in0=c_sb[:], in1=gain_all[:], op=MULT)
+                latent[u].append(c_sb)
+                gained[u].append(c_gain)
+
+        def root_mean_square(u):
+            total = work.tile([P, TILES], F32, name="sum_sq", bufs=3)
+            for i in range(TILES):
+                squares = work.tile([P, PACK, P], BF16)
+                nc.scalar.activation(
+                    out=squares[:], in_=latent[u][i][:], func=ACT.Square, accum_out=total[:, i : i + 1]
+                )
+            root = work.tile([P, TILES], F32, name="rms", bufs=3)
+            nc.scalar.activation(out=root[:], in_=total[:], func=ACT.Sqrt, bias=eps[:], scale=1.0 / RANK)
+            rms[u] = root
+
+        def invert_rms(u):
+            inverse = work.tile([P, TILES], F32, name="inv_rms", bufs=3)
+            nc.vector.reciprocal(out=inverse[:], in_=rms[u][:])
+            inv_rms[u] = inverse
+
+        def normalise_and_flip(u):
+            kvc_t = psum.tile([P, TILES, PACK, P], BF16)
+            for i in range(TILES):
+                kvc = work.tile([P, PACK, P], BF16, bufs=2 * TILES)
+                nc.scalar.activation(
+                    out=kvc[:], in_=gained[u][i][:], func=ACT.Copy, scale=inv_rms[u][:, i : i + 1]
+                )
+                for t in range(PACK):
+                    nc.tensor.transpose(kvc_t[:, i, t, :], kvc[:, t, :], ident_bf16[:])
+            kvc_flipped[u] = kvc_t
+
+        def copy_kvc(u):
+            grouped = work.tile([P, TILES, P, PACK], BF16, align_bytes=64, name="kvc_grouped")
+            nc.scalar.copy(out=grouped[:], in_=kvc_flipped[u][:].rearrange("p i t r -> p i r t"))
+            kvc_grouped[u] = grouped
+
+        def project_matmul(u):
+            kv_ps[u] = []
+            for i in range(TILES):
+                for b in range(KV // BANK):
+                    cols = slice(b * BANK, (b + 1) * BANK)
+                    bank = psum.tile([P, BANK], F32, name="kv_bank", bufs=TILES * KV // BANK)
+                    multiply(bank[:], kvc_mx[u], i, wb_words[:, cols], wb_plane[:, cols])
+                    kv_ps[u].append(bank)
+
+        def project_bias_and_store(u):
+            result = work.tile([P, 2, TILES, HEADS, HEAD_DIM], F32, bufs=4)
+            for i in range(TILES):
+                for b in range(KV // BANK):
+                    cols = slice(b * BANK, (b + 1) * BANK)
+                    nc.vector.tensor_tensor(
+                        out=result[:, :, i, 2 * b : 2 * b + 2, :].rearrange("p w h d -> p h w d"),
+                        in0=kv_ps[u][i * (KV // BANK) + b][:].rearrange("p (h w d) -> p h w d", h=2, w=2),
+                        in1=b2_all[:, cols].rearrange("p (h w d) -> p h w d", h=2, w=2),
+                        op=ADD,
+                    )
+            for w in range(2):
+                nc.sync.dma_start(out=out_units[w][u], in_=result[:, w].rearrange("p i h d -> p (i h d)"))
+
+        def live(u):
+            return 0 <= u < UNITS
+
+        for k in range(-3, UNITS + 3):
+            if live(k + 2):
+                copy_x(k + 2)
+            if live(k + 3):
+                flip_x(k + 3)
+            if live(k):
+                latent_bias_and_gain(k)
+            if live(k + 1):
+                latent_matmul(k + 1)
+            if live(k - 1):
+                normalise_and_flip(k - 1)
+            if live(k - 2):
+                kvc_mx[k - 2] = quantise(kvc_grouped[k - 2], "kvc", 2)
+            if live(k):
+                root_mean_square(k)
+            if live(k - 3):
+                project_bias_and_store(k - 3)
+            if live(k - 2):
+                project_matmul(k - 2)
+            if live(k - 1):
+                copy_kvc(k - 1)
+            if live(k):
+                invert_rms(k)
+            if live(k + 2):
+                x_mx[k + 2] = quantise(x_grouped[k + 2], "x", 3)

@@ -54,7 +54,6 @@ def tile_mla_pa_t_kernel(
         const = ctx.enter_context(tc.tile_pool(name="const", bufs=1))
         work = ctx.enter_context(tc.tile_pool(name="work", bufs=2))
         psum = ctx.enter_context(tc.psum_pool(name="psum", bufs=1))
-        ctx.enter_context(tc.manual_schedule())
 
         planes = const.tile([P, RANK + KV], U8, align_bytes=64)
         nc.vector.memset(planes[:].bitcast(I32), 0)
@@ -75,35 +74,46 @@ def tile_mla_pa_t_kernel(
                 in_=dram_words[0].rearrange("p n t -> p (n t)").bitcast(I32),
             )
 
+        nc.sync.dma_start(out=x_all[:, 0], in_=x_units[0])
         load_weight(wa_words, wa_plane, wkv_a_w_words, wkv_a_w_scales)
-        for u in range(2):
-            nc.sync.dma_start(out=x_all[:, u], in_=x_units[u])
+        nc.sync.dma_start(out=x_all[:, 1], in_=x_units[1])
         load_weight(wb_words, wb_plane, wkv_b_w_words, wkv_b_w_scales)
         for u in range(2, UNITS):
             nc.sync.dma_start(out=x_all[:, u], in_=x_units[u])
-
-        b1_raw = const.tile([P, RANK], BF16)
-        gain_raw = const.tile([P, RANK], BF16)
-        b2_all = const.tile([P, KV], BF16)
-        nc.scalar.dma_start(out=b1_raw[:], in_=wkv_a_b.partition_broadcast(P))
-        nc.scalar.dma_start(out=gain_raw[:], in_=kv_norm_w.partition_broadcast(P))
-        nc.scalar.dma_start(out=b2_all[:], in_=wkv_b_b.partition_broadcast(P))
-        eps = const.tile([P, 1], F32)
-        nc.vector.memset(eps[:], EPS)
-        warm = const.tile([P, 1], F32)
-        nc.scalar.activation(out=warm[:], in_=eps[:], func=ACT.Sqrt)
-        b1_all = const.tile([P, PACK, P], F32)
-        gain_all = const.tile([P, PACK, P], F32)
-        nc.vector.tensor_copy(out=b1_all[:], in_=b1_raw[:].rearrange("p (m t) -> p t m", t=PACK))
-        nc.vector.tensor_copy(out=gain_all[:], in_=gain_raw[:].rearrange("p (m t) -> p t m", t=PACK))
 
         ident_f32 = const.tile([P, P], F32)
         make_identity(nc, ident_f32[:])
         ident_bf16 = const.tile([P, P], BF16)
         make_identity(nc, ident_bf16[:])
 
+        rows = const.tile([P, RANK + RANK + KV], BF16)
+        nc.vector.memset(rows[:], 0.0)
+        ones = const.tile([P, P], BF16)
+        nc.vector.memset(ones[:], 1.0)
+        eps = const.tile([P, 1], F32)
+        nc.vector.memset(eps[:], EPS)
+        nc.scalar.dma_start(out=rows[0:1, 0:RANK], in_=wkv_a_b.unsqueeze(0))
+        nc.scalar.dma_start(out=rows[0:1, RANK : 2 * RANK], in_=kv_norm_w.unsqueeze(0))
+        nc.scalar.dma_start(out=rows[0:1, 2 * RANK :], in_=wkv_b_b.unsqueeze(0))
+        warm = const.tile([P, 1], F32)
+        nc.scalar.activation(out=warm[:], in_=eps[:], func=ACT.Sqrt)
+        spread = []
+        for b in range(4):
+            bank = psum.tile([P, BANK], F32, name="kv_bank", bufs=TILES * KV // BANK)
+            nc.tensor.matmul(
+                out=bank[:], lhsT=ones[:], rhs=rows[:, b * BANK : (b + 1) * BANK], start=True, stop=True
+            )
+            spread.append(bank)
+        b1_all = const.tile([P, PACK, P], F32)
+        gain_all = const.tile([P, PACK, P], F32)
+        b2_all = const.tile([P, KV], F32)
+        nc.vector.tensor_copy(out=b1_all[:], in_=spread[0][:].rearrange("p (m t) -> p t m", t=PACK))
+        nc.vector.tensor_copy(out=gain_all[:], in_=spread[1][:].rearrange("p (m t) -> p t m", t=PACK))
+        nc.scalar.copy(out=b2_all[:, 0:BANK], in_=spread[2][:])
+        nc.scalar.copy(out=b2_all[:, BANK:KV], in_=spread[3][:])
+
         x_flipped, x_grouped, x_mx = {}, {}, {}
-        latent_ps, latent, gained, rms, inv_rms = {}, {}, {}, {}, {}
+        latent_ps, latent, gained, sum_sq, rms, inv_rms = {}, {}, {}, {}, {}, {}
         kvc_flipped, kvc_grouped, kvc_mx, kv_ps = {}, {}, {}, {}
 
         def flip_x(u):
@@ -164,15 +174,18 @@ def tile_mla_pa_t_kernel(
                 latent[u].append(c_sb)
                 gained[u].append(c_gain)
 
+        def sum_squares(u, i):
+            if i == 0:
+                total = work.tile([P, TILES], F32, name="sum_sq", bufs=3)
+                sum_sq[u] = total
+            squares = work.tile([P, PACK, P], BF16)
+            nc.scalar.activation(
+                out=squares[:], in_=latent[u][i][:], func=ACT.Square, accum_out=sum_sq[u][:, i : i + 1]
+            )
+
         def root_mean_square(u):
-            total = work.tile([P, TILES], F32, name="sum_sq", bufs=3)
-            for i in range(TILES):
-                squares = work.tile([P, PACK, P], BF16)
-                nc.scalar.activation(
-                    out=squares[:], in_=latent[u][i][:], func=ACT.Square, accum_out=total[:, i : i + 1]
-                )
             root = work.tile([P, TILES], F32, name="rms", bufs=3)
-            nc.scalar.activation(out=root[:], in_=total[:], func=ACT.Sqrt, bias=eps[:], scale=1.0 / RANK)
+            nc.scalar.activation(out=root[:], in_=sum_sq[u][:], func=ACT.Sqrt, bias=eps[:], scale=1.0 / RANK)
             rms[u] = root
 
         def invert_rms(u):
@@ -188,7 +201,9 @@ def tile_mla_pa_t_kernel(
                     out=kvc[:], in_=gained[u][i][:], func=ACT.Copy, scale=inv_rms[u][:, i : i + 1]
                 )
                 for t in range(PACK):
-                    nc.tensor.transpose(kvc_t[:, i, t, :], kvc[:, t, :], ident_bf16[:])
+                    nc.tensor.matmul(
+                        out=kvc_t[:, i, t, :], lhsT=kvc[:, t, :], rhs=ident_bf16[:], start=True, stop=True
+                    )
             kvc_flipped[u] = kvc_t
 
         def copy_kvc(u):
@@ -236,6 +251,8 @@ def tile_mla_pa_t_kernel(
             if live(k - 2):
                 kvc_mx[k - 2] = quantise(kvc_grouped[k - 2], "kvc", 2)
             if live(k):
+                sum_squares(k, 0)
+                sum_squares(k, 1)
                 root_mean_square(k)
             if live(k - 3):
                 project_bias_and_store(k - 3)

@@ -54,6 +54,7 @@ def tile_mla_pa_t_kernel(
         const = ctx.enter_context(tc.tile_pool(name="const", bufs=1))
         work = ctx.enter_context(tc.tile_pool(name="work", bufs=2))
         psum = ctx.enter_context(tc.psum_pool(name="psum", bufs=1))
+        ctx.enter_context(tc.manual_schedule())
 
         planes = const.tile([P, RANK + KV], U8, align_bytes=64)
         nc.vector.memset(planes[:].bitcast(I32), 0)
@@ -96,7 +97,7 @@ def tile_mla_pa_t_kernel(
         nc.scalar.dma_start(out=rows[0:1, RANK : 2 * RANK], in_=kv_norm_w.unsqueeze(0))
         nc.scalar.dma_start(out=rows[0:1, 2 * RANK :], in_=wkv_b_b.unsqueeze(0))
         warm = const.tile([P, 1], F32)
-        nc.scalar.activation(out=warm[:], in_=eps[:], func=ACT.Sqrt)
+        nc.scalar.activation(out=warm[:], in_=eps[:], func=ACT.Abs_reciprocal_sqrt)
         spread = []
         for b in range(4):
             bank = psum.tile([P, BANK], F32, name="kv_bank", bufs=TILES * KV // BANK)
@@ -113,7 +114,7 @@ def tile_mla_pa_t_kernel(
         nc.scalar.copy(out=b2_all[:, BANK:KV], in_=spread[3][:])
 
         x_flipped, x_grouped, x_mx = {}, {}, {}
-        latent_ps, latent, gained, sum_sq, rms, inv_rms = {}, {}, {}, {}, {}, {}
+        latent_ps, latent, gained, sum_sq, inv_rms = {}, {}, {}, {}, {}
         kvc_flipped, kvc_grouped, kvc_mx, kv_ps = {}, {}, {}, {}
 
         def flip_x(u):
@@ -183,14 +184,11 @@ def tile_mla_pa_t_kernel(
                 out=squares[:], in_=latent[u][i][:], func=ACT.Square, accum_out=sum_sq[u][:, i : i + 1]
             )
 
-        def root_mean_square(u):
-            root = work.tile([P, TILES], F32, name="rms", bufs=3)
-            nc.scalar.activation(out=root[:], in_=sum_sq[u][:], func=ACT.Sqrt, bias=eps[:], scale=1.0 / RANK)
-            rms[u] = root
-
-        def invert_rms(u):
+        def inverse_rms(u):
             inverse = work.tile([P, TILES], F32, name="inv_rms", bufs=3)
-            nc.vector.reciprocal(out=inverse[:], in_=rms[u][:])
+            nc.scalar.activation(
+                out=inverse[:], in_=sum_sq[u][:], func=ACT.Abs_reciprocal_sqrt, bias=eps[:], scale=1.0 / RANK
+            )
             inv_rms[u] = inverse
 
         def normalise_and_flip(u):
@@ -244,23 +242,20 @@ def tile_mla_pa_t_kernel(
                 flip_x(k + 3)
             if live(k):
                 latent_bias_and_gain(k)
-            if live(k + 1):
-                latent_matmul(k + 1)
             if live(k - 1):
                 normalise_and_flip(k - 1)
-            if live(k - 2):
-                kvc_mx[k - 2] = quantise(kvc_grouped[k - 2], "kvc", 2)
+            if live(k + 1):
+                latent_matmul(k + 1)
             if live(k):
-                sum_squares(k, 0)
-                sum_squares(k, 1)
-                root_mean_square(k)
+                for i in range(TILES):
+                    sum_squares(k, i)
+                inverse_rms(k)
             if live(k - 3):
                 project_bias_and_store(k - 3)
-            if live(k - 2):
-                project_matmul(k - 2)
             if live(k - 1):
                 copy_kvc(k - 1)
-            if live(k):
-                invert_rms(k)
+            if live(k - 2):
+                kvc_mx[k - 2] = quantise(kvc_grouped[k - 2], "kvc", 2)
+                project_matmul(k - 2)
             if live(k + 2):
                 x_mx[k + 2] = quantise(x_grouped[k + 2], "x", 3)

@@ -46,7 +46,7 @@ def tile_mla_pa_t_kernel(
     nc = tc.nc
     x_units = x.flatten_outer_dims().rearrange("(u p i) d -> u p i d", p=P, i=TILES)
     out_units = [
-        o.rearrange("b s h d -> (b s) (h d)").rearrange("(u p i) c -> u p (i c)", p=P, i=TILES)
+        o.rearrange("b s h d -> (b s) (h d)").rearrange("(u p i) c -> u p i c", p=P, i=TILES)
         for o in (out_0, out_1)
     ]
 
@@ -98,20 +98,6 @@ def tile_mla_pa_t_kernel(
         nc.scalar.dma_start(out=rows[0:1, 2 * RANK :], in_=wkv_b_b.unsqueeze(0))
         warm = const.tile([P, 1], F32)
         nc.scalar.activation(out=warm[:], in_=eps[:], func=ACT.Abs_reciprocal_sqrt)
-        spread = []
-        for b in range(4):
-            bank = psum.tile([P, BANK], F32, name="kv_bank", bufs=TILES * KV // BANK)
-            nc.tensor.matmul(
-                out=bank[:], lhsT=ones[:], rhs=rows[:, b * BANK : (b + 1) * BANK], start=True, stop=True
-            )
-            spread.append(bank)
-        b1_all = const.tile([P, PACK, P], F32)
-        gain_all = const.tile([P, PACK, P], F32)
-        b2_all = const.tile([P, KV], F32)
-        nc.vector.tensor_copy(out=b1_all[:], in_=spread[0][:].rearrange("p (m t) -> p t m", t=PACK))
-        nc.vector.tensor_copy(out=gain_all[:], in_=spread[1][:].rearrange("p (m t) -> p t m", t=PACK))
-        nc.scalar.copy(out=b2_all[:, 0:BANK], in_=spread[2][:])
-        nc.scalar.copy(out=b2_all[:, BANK:KV], in_=spread[3][:])
 
         x_flipped, x_grouped, x_mx = {}, {}, {}
         latent_ps, latent, gained, sum_sq, inv_rms = {}, {}, {}, {}, {}
@@ -229,13 +215,34 @@ def tile_mla_pa_t_kernel(
                         in1=b2_all[:, cols].rearrange("p (h w d) -> p h w d", h=2, w=2),
                         op=ADD,
                     )
-            for w in range(2):
-                nc.sync.dma_start(out=out_units[w][u], in_=result[:, w].rearrange("p i h d -> p (i h d)"))
+                for w in range(2):
+                    nc.sync.dma_start(
+                        out=out_units[w][u][:, i, :], in_=result[:, w, i].rearrange("p h d -> p (h d)")
+                    )
 
         def live(u):
             return 0 <= u < UNITS
 
-        for k in range(-3, UNITS + 3):
+        flip_x(0)
+        copy_x(0)
+        flip_x(1)
+        x_mx[0] = quantise(x_grouped[0], "x", 3)
+        spread = []
+        for b in range(4):
+            bank = psum.tile([P, BANK], F32, name="kv_bank", bufs=TILES * KV // BANK)
+            nc.tensor.matmul(
+                out=bank[:], lhsT=ones[:], rhs=rows[:, b * BANK : (b + 1) * BANK], start=True, stop=True
+            )
+            spread.append(bank)
+        b1_all = const.tile([P, PACK, P], F32)
+        gain_all = const.tile([P, PACK, P], F32)
+        b2_all = const.tile([P, KV], F32)
+        nc.vector.tensor_copy(out=b1_all[:], in_=spread[0][:].rearrange("p (m t) -> p t m", t=PACK))
+        nc.vector.tensor_copy(out=gain_all[:], in_=spread[1][:].rearrange("p (m t) -> p t m", t=PACK))
+        nc.scalar.copy(out=b2_all[:, 0:BANK], in_=spread[2][:])
+        nc.scalar.copy(out=b2_all[:, BANK:KV], in_=spread[3][:])
+
+        for k in range(-1, UNITS + 3):
             if live(k + 2):
                 copy_x(k + 2)
             if live(k + 3):

@@ -84,8 +84,6 @@ def tile_mla_pa_t_kernel(
 
         ident_f32 = const.tile([P, P], F32)
         make_identity(nc, ident_f32[:])
-        ident_bf16 = const.tile([P, P], BF16)
-        make_identity(nc, ident_bf16[:])
 
         rows = const.tile([P, RANK + RANK + KV], BF16)
         nc.vector.memset(rows[:], 0.0)
@@ -149,14 +147,14 @@ def tile_mla_pa_t_kernel(
         def latent_bias_and_gain(u):
             latent[u], gained[u] = [], []
             for i in range(TILES):
-                c_sb = work.tile([P, PACK, P], F32, bufs=2 * TILES)
+                c_sb = work.tile([P, 2, P, 2], F32, bufs=2 * TILES)
                 nc.vector.tensor_tensor(
                     out=c_sb[:],
-                    in0=latent_ps[u][i][:].rearrange("p (m t) -> p t m", t=PACK),
+                    in0=latent_ps[u][i][:].rearrange("p (m h e) -> p h m e", h=2, e=2),
                     in1=b1_all[:],
                     op=ADD,
                 )
-                c_gain = work.tile([P, PACK, P], F32, bufs=3 * TILES)
+                c_gain = work.tile([P, 2, P, 2], F32, bufs=3 * TILES)
                 nc.gpsimd.tensor_tensor(out=c_gain[:], in0=c_sb[:], in1=gain_all[:], op=MULT)
                 latent[u].append(c_sb)
                 gained[u].append(c_gain)
@@ -165,7 +163,7 @@ def tile_mla_pa_t_kernel(
             if i == 0:
                 total = work.tile([P, TILES], F32, name="sum_sq", bufs=3)
                 sum_sq[u] = total
-            squares = work.tile([P, PACK, P], BF16)
+            squares = work.tile([P, 2, P, 2], BF16)
             nc.scalar.activation(
                 out=squares[:], in_=latent[u][i][:], func=ACT.Square, accum_out=sum_sq[u][:, i : i + 1]
             )
@@ -178,21 +176,20 @@ def tile_mla_pa_t_kernel(
             inv_rms[u] = inverse
 
         def normalise_and_flip(u):
-            kvc_t = psum.tile([P, TILES, PACK, P], BF16)
+            kvc_t = psum.tile([P, TILES, 2, P], F32)
             for i in range(TILES):
-                kvc = work.tile([P, PACK, P], BF16, bufs=2 * TILES)
+                kvc = work.tile([P, 2, P, 2], BF16, bufs=2 * TILES)
                 nc.scalar.activation(
                     out=kvc[:], in_=gained[u][i][:], func=ACT.Copy, scale=inv_rms[u][:, i : i + 1]
                 )
-                for t in range(PACK):
-                    nc.tensor.matmul(
-                        out=kvc_t[:, i, t, :], lhsT=kvc[:, t, :], rhs=ident_bf16[:], start=True, stop=True
-                    )
+                words = kvc[:].rearrange("p h m e -> p (h m e)").bitcast(F32)
+                for h in range(2):
+                    nc.tensor.transpose(kvc_t[:, i, h, :], words[:, h * P : (h + 1) * P], ident_f32[:])
             kvc_flipped[u] = kvc_t
 
         def copy_kvc(u):
             grouped = work.tile([P, TILES, P, PACK], BF16, align_bytes=64, name="kvc_grouped")
-            nc.scalar.copy(out=grouped[:], in_=kvc_flipped[u][:].rearrange("p i t r -> p i r t"))
+            nc.scalar.copy(out=grouped[:].bitcast(F32), in_=kvc_flipped[u][:].rearrange("p i h r -> p i r h"))
             kvc_grouped[u] = grouped
 
         def project_matmul(u):
@@ -234,11 +231,11 @@ def tile_mla_pa_t_kernel(
                 out=bank[:], lhsT=ones[:], rhs=rows[:, b * BANK : (b + 1) * BANK], start=True, stop=True
             )
             spread.append(bank)
-        b1_all = const.tile([P, PACK, P], F32)
-        gain_all = const.tile([P, PACK, P], F32)
+        b1_all = const.tile([P, 2, P, 2], F32)
+        gain_all = const.tile([P, 2, P, 2], F32)
         b2_all = const.tile([P, KV], F32)
-        nc.vector.tensor_copy(out=b1_all[:], in_=spread[0][:].rearrange("p (m t) -> p t m", t=PACK))
-        nc.vector.tensor_copy(out=gain_all[:], in_=spread[1][:].rearrange("p (m t) -> p t m", t=PACK))
+        nc.vector.tensor_copy(out=b1_all[:], in_=spread[0][:].rearrange("p (m h e) -> p h m e", h=2, e=2))
+        nc.vector.tensor_copy(out=gain_all[:], in_=spread[1][:].rearrange("p (m h e) -> p h m e", h=2, e=2))
         nc.scalar.copy(out=b2_all[:, 0:BANK], in_=spread[2][:])
         nc.scalar.copy(out=b2_all[:, BANK:KV], in_=spread[3][:])
 

@@ -24,8 +24,10 @@ KV = HEADS * 2 * HEAD_DIM
 BANK = 512
 EPS = 1e-6
 
-TILES = 2
-UNITS = TOKENS // (TILES * P)
+PAIR = 2
+LOADS = TOKENS // (PAIR * P)
+TILES = TOKENS // P
+AHEAD = 3
 
 FLOPS = 2 * TOKENS * (DIM * RANK + RANK * KV)
 
@@ -44,16 +46,16 @@ def tile_mla_pa_t_kernel(
     out_1,
 ):
     nc = tc.nc
-    x_units = x.flatten_outer_dims().rearrange("(u p i) d -> u p i d", p=P, i=TILES)
-    out_units = [
-        o.rearrange("b s h d -> (b s) (h d)").rearrange("(u p i) c -> u p i c", p=P, i=TILES)
+    x_pairs = x.flatten_outer_dims().rearrange("(u p i) d -> u p i d", p=P, i=PAIR)
+    out_pairs = [
+        o.rearrange("b s h d -> (b s) (h d)").rearrange("(u p i) c -> u p i c", p=P, i=PAIR)
         for o in (out_0, out_1)
     ]
 
     with ExitStack() as ctx:
         const = ctx.enter_context(tc.tile_pool(name="const", bufs=1))
-        work = ctx.enter_context(tc.tile_pool(name="work", bufs=2))
-        psum = ctx.enter_context(tc.psum_pool(name="psum", bufs=1))
+        work = ctx.enter_context(tc.tile_pool(name="work", bufs=3))
+        psum = ctx.enter_context(tc.psum_pool(name="psum", bufs=2))
         ctx.enter_context(tc.manual_schedule())
 
         planes = const.tile([P, RANK + KV], U8, align_bytes=64)
@@ -62,7 +64,7 @@ def tile_mla_pa_t_kernel(
         wb_plane = planes[:, RANK : RANK + KV]
         wa_words = const.tile([P, RANK], U32, align_bytes=64)
         wb_words = const.tile([P, KV], U32, align_bytes=64)
-        x_all = const.tile([P, UNITS, TILES, DIM], BF16)
+        x_all = const.tile([P, LOADS, PAIR, DIM], BF16)
 
         def load_weight(words, plane, dram_words, dram_scales):
             for q in range(4):
@@ -75,12 +77,12 @@ def tile_mla_pa_t_kernel(
                 in_=dram_words[0].rearrange("p n t -> p (n t)").bitcast(I32),
             )
 
-        nc.sync.dma_start(out=x_all[:, 0], in_=x_units[0])
+        nc.sync.dma_start(out=x_all[:, 0], in_=x_pairs[0])
         load_weight(wa_words, wa_plane, wkv_a_w_words, wkv_a_w_scales)
-        nc.sync.dma_start(out=x_all[:, 1], in_=x_units[1])
+        nc.sync.dma_start(out=x_all[:, 1], in_=x_pairs[1])
         load_weight(wb_words, wb_plane, wkv_b_w_words, wkv_b_w_scales)
-        for u in range(2, UNITS):
-            nc.sync.dma_start(out=x_all[:, u], in_=x_units[u])
+        for u in range(2, LOADS):
+            nc.sync.dma_start(out=x_all[:, u], in_=x_pairs[u])
 
         ident_f32 = const.tile([P, P], F32)
         make_identity(nc, ident_f32[:])
@@ -97,36 +99,69 @@ def tile_mla_pa_t_kernel(
         warm = const.tile([P, 1], F32)
         nc.scalar.activation(out=warm[:], in_=eps[:], func=ACT.Abs_reciprocal_sqrt)
 
-        x_flipped, x_grouped, x_mx = {}, {}, {}
-        latent_ps, latent, gained, sum_sq, inv_rms = {}, {}, {}, {}, {}
-        kvc_flipped, kvc_grouped, kvc_mx, kv_ps = {}, {}, {}, {}
+        b1_all = const.tile([P, 2, P, 2], F32)
+        gain_all = const.tile([P, 2, P, 2], F32)
+        b2_all = const.tile([P, KV], F32)
 
-        def flip_x(u):
-            x_t = psum.tile([P, TILES, 2, P], F32)
-            for i in range(TILES):
-                words = x_all[:, u, i, :].bitcast(F32)
-                for h in range(2):
-                    nc.tensor.transpose(x_t[:, i, h, :], words[:, h : DIM // 2 : 2], ident_f32[:])
-            x_flipped[u] = x_t
-
-        def copy_x(u):
-            grouped = work.tile([P, TILES, P, PACK], BF16, align_bytes=64, name="x_grouped")
-            nc.scalar.copy(out=grouped[:].bitcast(F32), in_=x_flipped[u][:].rearrange("p i h r -> p i r h"))
-            x_grouped[u] = grouped
-
-        def quantise(grouped, name, bufs):
-            codes = work.tile([P, TILES * P], U32, align_bytes=64, name=name + "_codes", bufs=bufs)
-            plane = work.tile([P, TILES * P], U8, align_bytes=64, name=name + "_plane", bufs=bufs)
-            nc.vector.quantize_mx(
-                out=codes[:].bitcast(FP8X4),
-                scales=plane[:],
-                in_=grouped[:].rearrange("p i r t -> p (i r t)"),
+        def spread(b):
+            bank = psum.tile([P, BANK], F32, name="kv_bank", bufs=4)
+            nc.tensor.matmul(
+                out=bank[:], lhsT=ones[:], rhs=rows[:, b * BANK : (b + 1) * BANK], start=True, stop=True
             )
-            return codes, plane
+            return bank
 
-        def multiply(out, mx, i, words, plane):
-            codes, scales = mx
-            tok = slice(i * P, (i + 1) * P)
+        flipped, grouped, x_mx, kvc_mx = {}, {}, {}, {}
+        latent_ps, latent, gained, sum_sq, inv_rms, kvc, kv_ps = {}, {}, {}, {}, {}, {}, {}
+
+        def live(j):
+            return 0 <= j < TILES
+
+        def halves(n):
+            return (0 if live(n + AHEAD) else 1), (2 if live(n - 1) else 1)
+
+        def flip(n):
+            lo, hi = halves(n)
+            if lo >= hi:
+                return
+            bank = psum.tile([P, 2, 2, P], F32, name="flipped")
+            if live(n + AHEAD):
+                j = n + AHEAD
+                words = x_all[:, j // PAIR, j % PAIR, :].bitcast(F32)
+                for h in range(2):
+                    nc.tensor.transpose(bank[:, 0, h, :], words[:, h : DIM // 2 : 2], ident_f32[:])
+            if live(n - 1):
+                words = kvc[n - 1][:].rearrange("p h m e -> p (h m e)").bitcast(F32)
+                for h in range(2):
+                    nc.tensor.transpose(bank[:, 1, h, :], words[:, h * P : (h + 1) * P], ident_f32[:])
+            flipped[n] = bank
+
+        def copy_out(n):
+            lo, hi = halves(n)
+            if lo >= hi:
+                return
+            tile = work.tile([P, 2, P, PACK], BF16, align_bytes=64, name="grouped")
+            nc.scalar.copy(
+                out=tile[:, lo:hi].bitcast(F32), in_=flipped[n][:, lo:hi].rearrange("p s h r -> p s r h")
+            )
+            grouped[n] = tile
+
+        def quantise(n):
+            lo, hi = halves(n - 1)
+            if lo >= hi:
+                return
+            codes = work.tile([P, 2 * P], U32, align_bytes=64, name="codes", bufs=4)
+            plane = work.tile([P, 2 * P], U8, align_bytes=64, name="plane", bufs=4)
+            cols = slice(lo * P, hi * P)
+            nc.vector.quantize_mx(
+                out=codes[:, cols].bitcast(FP8X4),
+                scales=plane[:, cols],
+                in_=grouped[n - 1][:, lo:hi].rearrange("p s r t -> p (s r t)"),
+            )
+            x_mx[n - 1 + AHEAD] = (codes, plane, slice(0, P))
+            kvc_mx[n - 2] = (codes, plane, slice(P, 2 * P))
+
+        def multiply(out, mx, words, plane):
+            codes, scales, tok = mx
             nc.tensor.matmul_mx(
                 out=out,
                 lhsT=codes[:, tok].bitcast(FP8X4),
@@ -137,129 +172,95 @@ def tile_mla_pa_t_kernel(
                 stop=True,
             )
 
-        def latent_matmul(u):
-            latent_ps[u] = []
-            for i in range(TILES):
-                c_ps = psum.tile([P, RANK], F32, bufs=TILES)
-                multiply(c_ps[:], x_mx[u], i, wa_words[:], wa_plane)
-                latent_ps[u].append(c_ps)
+        def latent_matmul(j):
+            if not live(j):
+                return
+            c_ps = psum.tile([P, RANK], F32, name="c_ps")
+            multiply(c_ps[:], x_mx[j], wa_words[:], wa_plane)
+            latent_ps[j] = c_ps
 
-        def latent_bias_and_gain(u):
-            latent[u], gained[u] = [], []
-            for i in range(TILES):
-                c_sb = work.tile([P, 2, P, 2], F32, bufs=2 * TILES)
+        def latent_bias(j):
+            if not live(j):
+                return
+            c_sb = work.tile([P, 2, P, 2], F32, name="c_sb")
+            nc.vector.tensor_tensor(
+                out=c_sb[:],
+                in0=latent_ps[j][:].rearrange("p (m h e) -> p h m e", h=2, e=2),
+                in1=b1_all[:],
+                op=ADD,
+            )
+            latent[j] = c_sb
+
+        def gain(j):
+            if not live(j):
+                return
+            c_gain = work.tile([P, 2, P, 2], F32, name="c_gain")
+            nc.gpsimd.tensor_tensor(out=c_gain[:], in0=latent[j][:], in1=gain_all[:], op=MULT)
+            gained[j] = c_gain
+
+        def inverse_rms(j):
+            if not live(j):
+                return
+            total = work.tile([P, 1], F32, name="sum_sq")
+            squares = work.tile([P, 2, P, 2], BF16, name="squares", bufs=2)
+            nc.scalar.activation(out=squares[:], in_=latent[j][:], func=ACT.Square, accum_out=total[:])
+            inverse = work.tile([P, 1], F32, name="inv_rms")
+            nc.scalar.activation(
+                out=inverse[:], in_=total[:], func=ACT.Abs_reciprocal_sqrt, bias=eps[:], scale=1.0 / RANK
+            )
+            inv_rms[j] = inverse
+
+        def normalise(j):
+            if not live(j):
+                return
+            tile = work.tile([P, 2, P, 2], BF16, name="kvc")
+            nc.scalar.activation(out=tile[:], in_=gained[j][:], func=ACT.Copy, scale=inv_rms[j][:])
+            kvc[j] = tile
+
+        def project_matmul(j):
+            if not live(j):
+                return
+            kv_ps[j] = []
+            for b in range(KV // BANK):
+                cols = slice(b * BANK, (b + 1) * BANK)
+                bank = psum.tile([P, BANK], F32, name="kv_bank", bufs=4)
+                multiply(bank[:], kvc_mx[j], wb_words[:, cols], wb_plane[:, cols])
+                kv_ps[j].append(bank)
+
+        def project_bias_and_store(j):
+            if not live(j):
+                return
+            result = work.tile([P, 2, HEADS, HEAD_DIM], F32, name="result", bufs=8)
+            for b in range(KV // BANK):
+                cols = slice(b * BANK, (b + 1) * BANK)
                 nc.vector.tensor_tensor(
-                    out=c_sb[:],
-                    in0=latent_ps[u][i][:].rearrange("p (m h e) -> p h m e", h=2, e=2),
-                    in1=b1_all[:],
+                    out=result[:, :, 2 * b : 2 * b + 2, :].rearrange("p w h d -> p h w d"),
+                    in0=kv_ps[j][b][:].rearrange("p (h w d) -> p h w d", h=2, w=2),
+                    in1=b2_all[:, cols].rearrange("p (h w d) -> p h w d", h=2, w=2),
                     op=ADD,
                 )
-                c_gain = work.tile([P, 2, P, 2], F32, bufs=3 * TILES)
-                nc.gpsimd.tensor_tensor(out=c_gain[:], in0=c_sb[:], in1=gain_all[:], op=MULT)
-                latent[u].append(c_sb)
-                gained[u].append(c_gain)
-
-        def sum_squares(u, i):
-            if i == 0:
-                total = work.tile([P, TILES], F32, name="sum_sq", bufs=3)
-                sum_sq[u] = total
-            squares = work.tile([P, 2, P, 2], BF16)
-            nc.scalar.activation(
-                out=squares[:], in_=latent[u][i][:], func=ACT.Square, accum_out=sum_sq[u][:, i : i + 1]
-            )
-
-        def inverse_rms(u):
-            inverse = work.tile([P, TILES], F32, name="inv_rms", bufs=3)
-            nc.scalar.activation(
-                out=inverse[:], in_=sum_sq[u][:], func=ACT.Abs_reciprocal_sqrt, bias=eps[:], scale=1.0 / RANK
-            )
-            inv_rms[u] = inverse
-
-        def normalise_and_flip(u):
-            kvc_t = psum.tile([P, TILES, 2, P], F32)
-            for i in range(TILES):
-                kvc = work.tile([P, 2, P, 2], BF16, bufs=2 * TILES)
-                nc.scalar.activation(
-                    out=kvc[:], in_=gained[u][i][:], func=ACT.Copy, scale=inv_rms[u][:, i : i + 1]
+            for w in range(2):
+                nc.sync.dma_start(
+                    out=out_pairs[w][j // PAIR][:, j % PAIR, :], in_=result[:, w].rearrange("p h d -> p (h d)")
                 )
-                words = kvc[:].rearrange("p h m e -> p (h m e)").bitcast(F32)
-                for h in range(2):
-                    nc.tensor.transpose(kvc_t[:, i, h, :], words[:, h * P : (h + 1) * P], ident_f32[:])
-            kvc_flipped[u] = kvc_t
 
-        def copy_kvc(u):
-            grouped = work.tile([P, TILES, P, PACK], BF16, align_bytes=64, name="kvc_grouped")
-            nc.scalar.copy(out=grouped[:].bitcast(F32), in_=kvc_flipped[u][:].rearrange("p i h r -> p i r h"))
-            kvc_grouped[u] = grouped
-
-        def project_matmul(u):
-            kv_ps[u] = []
-            for i in range(TILES):
-                for b in range(KV // BANK):
-                    cols = slice(b * BANK, (b + 1) * BANK)
-                    bank = psum.tile([P, BANK], F32, name="kv_bank", bufs=TILES * KV // BANK)
-                    multiply(bank[:], kvc_mx[u], i, wb_words[:, cols], wb_plane[:, cols])
-                    kv_ps[u].append(bank)
-
-        def project_bias_and_store(u):
-            result = work.tile([P, 2, TILES, HEADS, HEAD_DIM], F32, bufs=4)
-            for i in range(TILES):
-                for b in range(KV // BANK):
-                    cols = slice(b * BANK, (b + 1) * BANK)
-                    nc.vector.tensor_tensor(
-                        out=result[:, :, i, 2 * b : 2 * b + 2, :].rearrange("p w h d -> p h w d"),
-                        in0=kv_ps[u][i * (KV // BANK) + b][:].rearrange("p (h w d) -> p h w d", h=2, w=2),
-                        in1=b2_all[:, cols].rearrange("p (h w d) -> p h w d", h=2, w=2),
-                        op=ADD,
-                    )
-                for w in range(2):
-                    nc.sync.dma_start(
-                        out=out_units[w][u][:, i, :], in_=result[:, w, i].rearrange("p h d -> p (h d)")
-                    )
-
-        def live(u):
-            return 0 <= u < UNITS
-
-        flip_x(0)
-        copy_x(0)
-        flip_x(1)
-        x_mx[0] = quantise(x_grouped[0], "x", 3)
-        spread = []
-        for b in range(4):
-            bank = psum.tile([P, BANK], F32, name="kv_bank", bufs=TILES * KV // BANK)
-            nc.tensor.matmul(
-                out=bank[:], lhsT=ones[:], rhs=rows[:, b * BANK : (b + 1) * BANK], start=True, stop=True
-            )
-            spread.append(bank)
-        b1_all = const.tile([P, 2, P, 2], F32)
-        gain_all = const.tile([P, 2, P, 2], F32)
-        b2_all = const.tile([P, KV], F32)
-        nc.vector.tensor_copy(out=b1_all[:], in_=spread[0][:].rearrange("p (m h e) -> p h m e", h=2, e=2))
-        nc.vector.tensor_copy(out=gain_all[:], in_=spread[1][:].rearrange("p (m h e) -> p h m e", h=2, e=2))
-        nc.scalar.copy(out=b2_all[:, 0:BANK], in_=spread[2][:])
-        nc.scalar.copy(out=b2_all[:, BANK:KV], in_=spread[3][:])
-
-        for k in range(-1, UNITS + 3):
-            if live(k + 2):
-                copy_x(k + 2)
-            if live(k + 3):
-                flip_x(k + 3)
-            if live(k):
-                latent_bias_and_gain(k)
-            if live(k - 1):
-                normalise_and_flip(k - 1)
-            if live(k + 1):
-                latent_matmul(k + 1)
-            if live(k):
-                for i in range(TILES):
-                    sum_squares(k, i)
-                inverse_rms(k)
-            if live(k - 3):
-                project_bias_and_store(k - 3)
-            if live(k - 1):
-                copy_kvc(k - 1)
-            if live(k - 2):
-                kvc_mx[k - 2] = quantise(kvc_grouped[k - 2], "kvc", 2)
-                project_matmul(k - 2)
-            if live(k + 2):
-                x_mx[k + 2] = quantise(x_grouped[k + 2], "x", 3)
+        for n in range(-AHEAD, TILES + 3):
+            latent_matmul(n + 1)
+            flip(n)
+            if n == -AHEAD:
+                b1_ps = spread(0)
+                gain_ps = spread(1)
+                nc.vector.tensor_copy(out=b1_all[:], in_=b1_ps[:].rearrange("p (m h e) -> p h m e", h=2, e=2))
+            latent_bias(n)
+            quantise(n)
+            gain(n)
+            project_matmul(n - 2)
+            inverse_rms(n)
+            copy_out(n)
+            if n == -AHEAD:
+                nc.scalar.copy(out=gain_all[:], in_=gain_ps[:].rearrange("p (m h e) -> p h m e", h=2, e=2))
+            normalise(n)
+            project_bias_and_store(n - 3)
+            if n in (0, 1):
+                b2_ps = spread(2 + n)
+                nc.vector.tensor_copy(out=b2_all[:, n * BANK : (n + 1) * BANK], in_=b2_ps[:])

@@ -28,6 +28,7 @@ PAIR = 2
 LOADS = TOKENS // (PAIR * P)
 TILES = TOKENS // P
 AHEAD = 3
+BEHIND = 2
 
 FLOPS = 2 * TOKENS * (DIM * RANK + RANK * KV)
 
@@ -117,7 +118,7 @@ def tile_mla_pa_t_kernel(
             return 0 <= j < TILES
 
         def halves(n):
-            return (0 if live(n + AHEAD) else 1), (2 if live(n - 1) else 1)
+            return (0 if live(n + AHEAD) else 1), (2 if live(n - BEHIND) else 1)
 
         def flip(n):
             lo, hi = halves(n)
@@ -129,8 +130,8 @@ def tile_mla_pa_t_kernel(
                 words = x_all[:, j // PAIR, j % PAIR, :].bitcast(F32)
                 for h in range(2):
                     nc.tensor.transpose(bank[:, 0, h, :], words[:, h : DIM // 2 : 2], ident_f32[:])
-            if live(n - 1):
-                words = kvc[n - 1][:].rearrange("p h m e -> p (h m e)").bitcast(F32)
+            if live(n - BEHIND):
+                words = kvc[n - BEHIND][:].rearrange("p h m e -> p (h m e)").bitcast(F32)
                 for h in range(2):
                     nc.tensor.transpose(bank[:, 1, h, :], words[:, h * P : (h + 1) * P], ident_f32[:])
             flipped[n] = bank
@@ -158,7 +159,7 @@ def tile_mla_pa_t_kernel(
                 in_=grouped[n - 1][:, lo:hi].rearrange("p s r t -> p (s r t)"),
             )
             x_mx[n - 1 + AHEAD] = (codes, plane, slice(0, P))
-            kvc_mx[n - 2] = (codes, plane, slice(P, 2 * P))
+            kvc_mx[n - 1 - BEHIND] = (codes, plane, slice(P, 2 * P))
 
         def multiply(out, mx, words, plane):
             codes, scales, tok = mx
@@ -182,7 +183,7 @@ def tile_mla_pa_t_kernel(
         def latent_bias(j):
             if not live(j):
                 return
-            c_sb = work.tile([P, 2, P, 2], F32, name="c_sb")
+            c_sb = work.tile([P, 2, P, 2], F32, name="c_sb", bufs=4)
             nc.vector.tensor_tensor(
                 out=c_sb[:],
                 in0=latent_ps[j][:].rearrange("p (m h e) -> p h m e", h=2, e=2),
@@ -194,7 +195,7 @@ def tile_mla_pa_t_kernel(
         def gain(j):
             if not live(j):
                 return
-            c_gain = work.tile([P, 2, P, 2], F32, name="c_gain")
+            c_gain = work.tile([P, 2, P, 2], F32, name="c_gain", bufs=4)
             nc.gpsimd.tensor_tensor(out=c_gain[:], in0=latent[j][:], in1=gain_all[:], op=MULT)
             gained[j] = c_gain
 
@@ -244,7 +245,7 @@ def tile_mla_pa_t_kernel(
                     out=out_pairs[w][j // PAIR][:, j % PAIR, :], in_=result[:, w].rearrange("p h d -> p (h d)")
                 )
 
-        for n in range(-AHEAD, TILES + 3):
+        for n in range(-AHEAD, TILES + BEHIND + 2):
             latent_matmul(n + 1)
             flip(n)
             if n == -AHEAD:
@@ -254,13 +255,13 @@ def tile_mla_pa_t_kernel(
             latent_bias(n)
             quantise(n)
             gain(n)
-            project_matmul(n - 2)
-            inverse_rms(n)
+            project_matmul(n - 1 - BEHIND)
+            inverse_rms(n - 1)
             copy_out(n)
             if n == -AHEAD:
                 nc.scalar.copy(out=gain_all[:], in_=gain_ps[:].rearrange("p (m h e) -> p h m e", h=2, e=2))
-            normalise(n)
-            project_bias_and_store(n - 3)
+            normalise(n - 1)
+            project_bias_and_store(n - 2 - BEHIND)
             if n in (0, 1):
                 b2_ps = spread(2 + n)
                 nc.vector.tensor_copy(out=b2_all[:, n * BANK : (n + 1) * BANK], in_=b2_ps[:])

@@ -29,6 +29,7 @@ LOADS = TOKENS // (PAIR * P)
 TILES = TOKENS // P
 AHEAD = 3
 BEHIND = 2
+WARM_UP = 14
 
 FLOPS = 2 * TOKENS * (DIM * RANK + RANK * KV)
 
@@ -60,7 +61,6 @@ def tile_mla_pa_t_kernel(
         ctx.enter_context(tc.manual_schedule())
 
         planes = const.tile([P, RANK + KV], U8, align_bytes=64)
-        nc.vector.memset(planes[:].bitcast(I32), 0)
         wa_plane = planes[:, 0:RANK]
         wb_plane = planes[:, RANK : RANK + KV]
         wa_words = const.tile([P, RANK], U32, align_bytes=64)
@@ -78,27 +78,30 @@ def tile_mla_pa_t_kernel(
                 in_=dram_words[0].rearrange("p n t -> p (n t)").bitcast(I32),
             )
 
-        nc.sync.dma_start(out=x_all[:, 0], in_=x_pairs[0])
+        rows = const.tile([P, RANK + RANK + KV], BF16)
+        ones = const.tile([P, P], BF16)
+        eps = const.tile([P, 1], F32)
+        nc.vector.memset(eps[:], EPS)
+        nc.vector.memset(rows[:, 0:RANK], 0.0)
+        nc.vector.memset(planes[:].bitcast(I32), 0)
+        nc.vector.memset(ones[:], 1.0)
+        nc.vector.memset(rows[:, RANK:], 0.0)
+        warm = const.tile([P, 1], F32)
+        nc.scalar.activation(out=warm[:], in_=eps[:], func=ACT.Abs_reciprocal_sqrt)
+
+        nc.sync.dma_start(out=x_all[:, 0, 0], in_=x_pairs[0][:, 0])
+        nc.sync.dma_start(out=rows[0:1, 0:RANK], in_=wkv_a_b.unsqueeze(0))
         load_weight(wa_words, wa_plane, wkv_a_w_words, wkv_a_w_scales)
+        nc.sync.dma_start(out=x_all[:, 0, 1], in_=x_pairs[0][:, 1])
+        nc.sync.dma_start(out=rows[0:1, RANK : 2 * RANK], in_=kv_norm_w.unsqueeze(0))
         nc.sync.dma_start(out=x_all[:, 1], in_=x_pairs[1])
         load_weight(wb_words, wb_plane, wkv_b_w_words, wkv_b_w_scales)
+        nc.sync.dma_start(out=rows[0:1, 2 * RANK :], in_=wkv_b_b.unsqueeze(0))
         for u in range(2, LOADS):
             nc.sync.dma_start(out=x_all[:, u], in_=x_pairs[u])
 
         ident_f32 = const.tile([P, P], F32)
         make_identity(nc, ident_f32[:])
-
-        rows = const.tile([P, RANK + RANK + KV], BF16)
-        nc.vector.memset(rows[:], 0.0)
-        ones = const.tile([P, P], BF16)
-        nc.vector.memset(ones[:], 1.0)
-        eps = const.tile([P, 1], F32)
-        nc.vector.memset(eps[:], EPS)
-        nc.scalar.dma_start(out=rows[0:1, 0:RANK], in_=wkv_a_b.unsqueeze(0))
-        nc.scalar.dma_start(out=rows[0:1, RANK : 2 * RANK], in_=kv_norm_w.unsqueeze(0))
-        nc.scalar.dma_start(out=rows[0:1, 2 * RANK :], in_=wkv_b_b.unsqueeze(0))
-        warm = const.tile([P, 1], F32)
-        nc.scalar.activation(out=warm[:], in_=eps[:], func=ACT.Abs_reciprocal_sqrt)
 
         b1_all = const.tile([P, 2, P, 2], F32)
         gain_all = const.tile([P, 2, P, 2], F32)
@@ -110,6 +113,10 @@ def tile_mla_pa_t_kernel(
                 out=bank[:], lhsT=ones[:], rhs=rows[:, b * BANK : (b + 1) * BANK], start=True, stop=True
             )
             return bank
+
+        idle_ps = psum.tile([P, BANK], F32, name="kv_bank", bufs=4)
+        for unused in range(WARM_UP):
+            nc.tensor.matmul(out=idle_ps[:, 0:P], lhsT=ones[:], rhs=ones[:], start=True, stop=True)
 
         flipped, grouped, x_mx, kvc_mx = {}, {}, {}, {}
         latent_ps, latent, gained, sum_sq, inv_rms, kvc, kv_ps = {}, {}, {}, {}, {}, {}, {}

@@ -68,30 +68,31 @@ def tile_mla_pa_t_kernel(
         x_all = const.tile([P, LOADS, PAIR, DIM], BF16)
 
         def load_weight(words, plane, dram_words, dram_scales):
+            nc.sync.dma_start(
+                out=words[:].bitcast(I32),
+                in_=dram_words[0].rearrange("p n t -> p (n t)").bitcast(I32),
+            )
             for q in range(4):
                 nc.sync.dma_start(
                     out=plane[32 * q : 32 * q + 4, :].bitcast(I32),
                     in_=dram_scales[0, 4 * q : 4 * q + 4, :].bitcast(I32),
                 )
-            nc.sync.dma_start(
-                out=words[:].bitcast(I32),
-                in_=dram_words[0].rearrange("p n t -> p (n t)").bitcast(I32),
-            )
 
         rows = const.tile([P, RANK + RANK + KV], BF16)
         ones = const.tile([P, P], BF16)
         eps = const.tile([P, 1], F32)
+        nc.vector.memset(wa_plane.bitcast(I32), 0)
         nc.vector.memset(eps[:], EPS)
         nc.vector.memset(rows[:, 0:RANK], 0.0)
-        nc.vector.memset(planes[:].bitcast(I32), 0)
         nc.vector.memset(ones[:], 1.0)
+        nc.vector.memset(wb_plane.bitcast(I32), 0)
         nc.vector.memset(rows[:, RANK:], 0.0)
         warm = const.tile([P, 1], F32)
         nc.scalar.activation(out=warm[:], in_=eps[:], func=ACT.Abs_reciprocal_sqrt)
 
         nc.sync.dma_start(out=x_all[:, 0, 0], in_=x_pairs[0][:, 0])
-        nc.sync.dma_start(out=rows[0:1, 0:RANK], in_=wkv_a_b.unsqueeze(0))
         load_weight(wa_words, wa_plane, wkv_a_w_words, wkv_a_w_scales)
+        nc.sync.dma_start(out=rows[0:1, 0:RANK], in_=wkv_a_b.unsqueeze(0))
         nc.sync.dma_start(out=x_all[:, 0, 1], in_=x_pairs[0][:, 1])
         nc.sync.dma_start(out=rows[0:1, RANK : 2 * RANK], in_=kv_norm_w.unsqueeze(0))
         nc.sync.dma_start(out=x_all[:, 1], in_=x_pairs[1])

@@ -81,24 +81,24 @@ def tile_mla_pa_t_kernel(
         rows = const.tile([P, RANK + RANK + KV], BF16)
         ones = const.tile([P, P], BF16)
         eps = const.tile([P, 1], F32)
-        nc.vector.memset(wa_plane.bitcast(I32), 0)
-        nc.vector.memset(eps[:], EPS)
-        nc.vector.memset(rows[:, 0:RANK], 0.0)
         nc.vector.memset(ones[:], 1.0)
+        nc.vector.memset(eps[:], EPS)
+        nc.vector.memset(wa_plane.bitcast(I32), 0)
+        nc.vector.memset(rows[:, 0 : 2 * RANK], 0.0)
         nc.vector.memset(wb_plane.bitcast(I32), 0)
-        nc.vector.memset(rows[:, RANK:], 0.0)
+        nc.vector.memset(rows[:, 2 * RANK :], 0.0)
         warm = const.tile([P, 1], F32)
         nc.scalar.activation(out=warm[:], in_=eps[:], func=ACT.Abs_reciprocal_sqrt)
 
-        nc.sync.dma_start(out=x_all[:, 0, 0], in_=x_pairs[0][:, 0])
+        nc.sync.dma_start(out=x_all[:, 0], in_=x_pairs[0])
         load_weight(wa_words, wa_plane, wkv_a_w_words, wkv_a_w_scales)
         nc.sync.dma_start(out=rows[0:1, 0:RANK], in_=wkv_a_b.unsqueeze(0))
-        nc.sync.dma_start(out=x_all[:, 0, 1], in_=x_pairs[0][:, 1])
         nc.sync.dma_start(out=rows[0:1, RANK : 2 * RANK], in_=kv_norm_w.unsqueeze(0))
         nc.sync.dma_start(out=x_all[:, 1], in_=x_pairs[1])
+        nc.sync.dma_start(out=x_all[:, 2], in_=x_pairs[2])
         load_weight(wb_words, wb_plane, wkv_b_w_words, wkv_b_w_scales)
         nc.sync.dma_start(out=rows[0:1, 2 * RANK :], in_=wkv_b_b.unsqueeze(0))
-        for u in range(2, LOADS):
+        for u in range(3, LOADS):
             nc.sync.dma_start(out=x_all[:, u], in_=x_pairs[u])
 
         ident_f32 = const.tile([P, P], F32)
@@ -256,20 +256,21 @@ def tile_mla_pa_t_kernel(
         for n in range(-AHEAD, TILES + BEHIND + 2):
             latent_matmul(n + 1)
             flip(n)
-            if n == -AHEAD:
+            if n == 1 - AHEAD:
                 b1_ps = spread(0)
                 gain_ps = spread(1)
-                nc.vector.tensor_copy(out=b1_all[:], in_=b1_ps[:].rearrange("p (m h e) -> p h m e", h=2, e=2))
             latent_bias(n)
             quantise(n)
+            if n == 1 - AHEAD:
+                nc.vector.tensor_copy(out=b1_all[:], in_=b1_ps[:].rearrange("p (m h e) -> p h m e", h=2, e=2))
             gain(n)
             project_matmul(n - 1 - BEHIND)
             inverse_rms(n - 1)
             copy_out(n)
-            if n == -AHEAD:
+            if n == 1 - AHEAD:
                 nc.scalar.copy(out=gain_all[:], in_=gain_ps[:].rearrange("p (m h e) -> p h m e", h=2, e=2))
             normalise(n - 1)
             project_bias_and_store(n - 2 - BEHIND)
-            if n in (0, 1):
-                b2_ps = spread(2 + n)
-                nc.vector.tensor_copy(out=b2_all[:, n * BANK : (n + 1) * BANK], in_=b2_ps[:])
+            if n in (1, 2):
+                b2_ps = spread(1 + n)
+                nc.vector.tensor_copy(out=b2_all[:, (n - 1) * BANK : n * BANK], in_=b2_ps[:])

@@ -240,7 +240,7 @@ def tile_mla_pa_t_kernel(
             if not live(j):
                 return
             result = work.tile([P, 2, HEADS, HEAD_DIM], F32, name="result", bufs=8)
-            for b in range(KV // BANK):
+            for b in reversed(range(KV // BANK)):
                 cols = slice(b * BANK, (b + 1) * BANK)
                 nc.vector.tensor_tensor(
                     out=result[:, :, 2 * b : 2 * b + 2, :].rearrange("p w h d -> p h w d"),

@@ -28,7 +28,7 @@ PAIR = 2
 LOADS = TOKENS // (PAIR * P)
 TILES = TOKENS // P
 AHEAD = 3
-BEHIND = 2
+BEHIND = 3
 WARM_UP = 14
 
 FLOPS = 2 * TOKENS * (DIM * RANK + RANK * KV)
@@ -207,15 +207,20 @@ def tile_mla_pa_t_kernel(
             nc.gpsimd.tensor_tensor(out=c_gain[:], in0=latent[j][:], in1=gain_all[:], op=MULT)
             gained[j] = c_gain
 
-        def inverse_rms(j):
+        def sum_squares(j):
             if not live(j):
                 return
             total = work.tile([P, 1], F32, name="sum_sq")
             squares = work.tile([P, 2, P, 2], BF16, name="squares", bufs=2)
             nc.scalar.activation(out=squares[:], in_=latent[j][:], func=ACT.Square, accum_out=total[:])
+            sum_sq[j] = total
+
+        def inverse_rms(j):
+            if not live(j):
+                return
             inverse = work.tile([P, 1], F32, name="inv_rms")
             nc.scalar.activation(
-                out=inverse[:], in_=total[:], func=ACT.Abs_reciprocal_sqrt, bias=eps[:], scale=1.0 / RANK
+                out=inverse[:], in_=sum_sq[j][:], func=ACT.Abs_reciprocal_sqrt, bias=eps[:], scale=1.0 / RANK
             )
             inv_rms[j] = inverse
 
@@ -254,8 +259,8 @@ def tile_mla_pa_t_kernel(
                 )
 
         for n in range(-AHEAD, TILES + BEHIND + 2):
-            latent_matmul(n + 1)
             flip(n)
+            latent_matmul(n + 1)
             if n == 1 - AHEAD:
                 b1_ps = spread(0)
                 gain_ps = spread(1)
@@ -265,11 +270,12 @@ def tile_mla_pa_t_kernel(
                 nc.vector.tensor_copy(out=b1_all[:], in_=b1_ps[:].rearrange("p (m h e) -> p h m e", h=2, e=2))
             gain(n)
             project_matmul(n - 1 - BEHIND)
-            inverse_rms(n - 1)
+            sum_squares(n - 1)
             copy_out(n)
             if n == 1 - AHEAD:
                 nc.scalar.copy(out=gain_all[:], in_=gain_ps[:].rearrange("p (m h e) -> p h m e", h=2, e=2))
-            normalise(n - 1)
+            normalise(n - 2)
+            inverse_rms(n - 1)
             project_bias_and_store(n - 2 - BEHIND)
             if n in (1, 2):
                 b2_ps = spread(1 + n)

@@ -93,8 +93,8 @@ def tile_mla_pa_t_kernel(
         nc.sync.dma_start(out=x_all[:, 0], in_=x_pairs[0])
         load_weight(wa_words, wa_plane, wkv_a_w_words, wkv_a_w_scales)
         nc.sync.dma_start(out=rows[0:1, 0:RANK], in_=wkv_a_b.unsqueeze(0))
-        nc.sync.dma_start(out=rows[0:1, RANK : 2 * RANK], in_=kv_norm_w.unsqueeze(0))
         nc.sync.dma_start(out=x_all[:, 1], in_=x_pairs[1])
+        nc.sync.dma_start(out=rows[0:1, RANK : 2 * RANK], in_=kv_norm_w.unsqueeze(0))
         nc.sync.dma_start(out=x_all[:, 2], in_=x_pairs[2])
         load_weight(wb_words, wb_plane, wkv_b_w_words, wkv_b_w_scales)
         nc.sync.dma_start(out=rows[0:1, 2 * RANK :], in_=wkv_b_b.unsqueeze(0))
@@ -263,20 +263,21 @@ def tile_mla_pa_t_kernel(
             latent_matmul(n + 1)
             if n == 1 - AHEAD:
                 b1_ps = spread(0)
-                gain_ps = spread(1)
             latent_bias(n)
             quantise(n)
             if n == 1 - AHEAD:
                 nc.vector.tensor_copy(out=b1_all[:], in_=b1_ps[:].rearrange("p (m h e) -> p h m e", h=2, e=2))
             gain(n)
             project_matmul(n - 1 - BEHIND)
+            if n == 2 - AHEAD:
+                gain_ps = spread(1)
             sum_squares(n - 1)
             copy_out(n)
-            if n == 1 - AHEAD:
+            if n == 2 - AHEAD:
                 nc.scalar.copy(out=gain_all[:], in_=gain_ps[:].rearrange("p (m h e) -> p h m e", h=2, e=2))
             normalise(n - 2)
             inverse_rms(n - 1)
             project_bias_and_store(n - 2 - BEHIND)
-            if n in (1, 2):
-                b2_ps = spread(1 + n)
-                nc.vector.tensor_copy(out=b2_all[:, (n - 1) * BANK : n * BANK], in_=b2_ps[:])
+            if n in (2, 3):
+                b2_ps = spread(n)
+                nc.vector.tensor_copy(out=b2_all[:, (n - 2) * BANK : (n - 1) * BANK], in_=b2_ps[:])

@@ -29,6 +29,7 @@ LOADS = TOKENS // (PAIR * P)
 TILES = TOKENS // P
 AHEAD = 3
 BEHIND = 3
+FILL = 2
 WARM_UP = 14
 
 FLOPS = 2 * TOKENS * (DIM * RANK + RANK * KV)
@@ -204,7 +205,8 @@ def tile_mla_pa_t_kernel(
             if not live(j):
                 return
             c_gain = work.tile([P, 2, P, 2], F32, name="c_gain", bufs=4)
-            nc.gpsimd.tensor_tensor(out=c_gain[:], in0=latent[j][:], in1=gain_all[:], op=MULT)
+            engine = nc.vector if j < FILL else nc.gpsimd
+            engine.tensor_tensor(out=c_gain[:], in0=latent[j][:], in1=gain_all[:], op=MULT)
             gained[j] = c_gain
 
         def sum_squares(j):

@@ -57,7 +57,7 @@ def tile_mla_pa_t_kernel(
 
     with ExitStack() as ctx:
         const = ctx.enter_context(tc.tile_pool(name="const", bufs=1))
-        work = ctx.enter_context(tc.tile_pool(name="work", bufs=3))
+        work = ctx.enter_context(tc.tile_pool(name="work", bufs=5))
         psum = ctx.enter_context(tc.psum_pool(name="psum", bufs=2))
         ctx.enter_context(tc.manual_schedule())
 
@@ -159,8 +159,8 @@ def tile_mla_pa_t_kernel(
             lo, hi = halves(n - 1)
             if lo >= hi:
                 return
-            codes = work.tile([P, 2 * P], U32, align_bytes=64, name="codes", bufs=4)
-            plane = work.tile([P, 2 * P], U8, align_bytes=64, name="plane", bufs=4)
+            codes = work.tile([P, 2 * P], U32, align_bytes=64, name="codes", bufs=6)
+            plane = work.tile([P, 2 * P], U8, align_bytes=64, name="plane", bufs=6)
             cols = slice(lo * P, hi * P)
             nc.vector.quantize_mx(
                 out=codes[:, cols].bitcast(FP8X4),
@@ -192,7 +192,7 @@ def tile_mla_pa_t_kernel(
         def latent_bias(j):
             if not live(j):
                 return
-            c_sb = work.tile([P, 2, P, 2], F32, name="c_sb", bufs=4)
+            c_sb = work.tile([P, 2, P, 2], F32, name="c_sb", bufs=6)
             nc.vector.tensor_tensor(
                 out=c_sb[:],
                 in0=latent_ps[j][:].rearrange("p (m h e) -> p h m e", h=2, e=2),
@@ -204,7 +204,7 @@ def tile_mla_pa_t_kernel(
         def gain(j):
             if not live(j):
                 return
-            c_gain = work.tile([P, 2, P, 2], F32, name="c_gain", bufs=4)
+            c_gain = work.tile([P, 2, P, 2], F32, name="c_gain", bufs=6)
             engine = nc.vector if j < FILL else nc.gpsimd
             engine.tensor_tensor(out=c_gain[:], in0=latent[j][:], in1=gain_all[:], op=MULT)
             gained[j] = c_gain
@@ -213,7 +213,7 @@ def tile_mla_pa_t_kernel(
             if not live(j):
                 return
             total = work.tile([P, 1], F32, name="sum_sq")
-            squares = work.tile([P, 2, P, 2], BF16, name="squares", bufs=2)
+            squares = work.tile([P, 2, P, 2], BF16, name="squares", bufs=4)
             nc.scalar.activation(out=squares[:], in_=latent[j][:], func=ACT.Square, accum_out=total[:])
             sum_sq[j] = total
 
@@ -246,7 +246,7 @@ def tile_mla_pa_t_kernel(
         def project_bias_and_store(j):
             if not live(j):
                 return
-            result = work.tile([P, 2, HEADS, HEAD_DIM], F32, name="result", bufs=8)
+            result = work.tile([P, 2, HEADS, HEAD_DIM], F32, name="result", bufs=32)
             for b in reversed(range(KV // BANK)):
                 cols = slice(b * BANK, (b + 1) * BANK)
                 nc.vector.tensor_tensor(
@@ -275,10 +275,10 @@ def tile_mla_pa_t_kernel(
                 gain_ps = spread(1)
             sum_squares(n - 1)
             copy_out(n)
+            inverse_rms(n - 1)
             if n == 2 - AHEAD:
                 nc.scalar.copy(out=gain_all[:], in_=gain_ps[:].rearrange("p (m h e) -> p h m e", h=2, e=2))
             normalise(n - 2)
-            inverse_rms(n - 1)
             project_bias_and_store(n - 2 - BEHIND)
             if n in (2, 3):
                 b2_ps = spread(n)

from contextlib import ExitStack

import concourse.mybir as mybir
from concourse.masks import make_identity

F32 = mybir.dt.float32
BF16 = mybir.dt.bfloat16
I32 = mybir.dt.int32
U32 = mybir.dt.uint32
U8 = mybir.dt.uint8
FP8X4 = mybir.dt.float8_e4m3fn_x4
ADD = mybir.AluOpType.add
MULT = mybir.AluOpType.mult
ACT = mybir.ActivationFunctionType

P = 128
PACK = 4
TOKENS = 2 * 2048
DIM = 512
RANK = 512
HEADS = 4
HEAD_DIM = 128
KV = HEADS * 2 * HEAD_DIM
BANK = 512
EPS = 1e-6

PAIR = 2
LOADS = TOKENS // (PAIR * P)
TILES = TOKENS // P
AHEAD = 3
BEHIND = 3
FILL = 2
WARM_UP = 14

FLOPS = 2 * TOKENS * (DIM * RANK + RANK * KV)


def tile_mla_pa_t_kernel(
    tc,
    x,
    wkv_a_w_words,
    wkv_a_w_scales,
    wkv_a_b,
    kv_norm_w,
    wkv_b_w_words,
    wkv_b_w_scales,
    wkv_b_b,
    out_0,
    out_1,
):
    nc = tc.nc
    x_pairs = x.flatten_outer_dims().rearrange("(u p i) d -> u p i d", p=P, i=PAIR)
    out_pairs = [
        o.rearrange("b s h d -> (b s) (h d)").rearrange("(u p i) c -> u p i c", p=P, i=PAIR)
        for o in (out_0, out_1)
    ]

    with ExitStack() as ctx:
        const = ctx.enter_context(tc.tile_pool(name="const", bufs=1))
        work = ctx.enter_context(tc.tile_pool(name="work", bufs=5))
        psum = ctx.enter_context(tc.psum_pool(name="psum", bufs=2))
        ctx.enter_context(tc.manual_schedule())

        planes = const.tile([P, RANK + KV], U8, align_bytes=64)
        wa_plane = planes[:, 0:RANK]
        wb_plane = planes[:, RANK : RANK + KV]
        wa_words = const.tile([P, RANK], U32, align_bytes=64)
        wb_words = const.tile([P, KV], U32, align_bytes=64)
        x_all = const.tile([P, LOADS, PAIR, DIM], BF16)

        def load_weight(words, plane, dram_words, dram_scales):
            nc.sync.dma_start(
                out=words[:].bitcast(I32),
                in_=dram_words[0].rearrange("p n t -> p (n t)").bitcast(I32),
            )
            for q in range(4):
                nc.sync.dma_start(
                    out=plane[32 * q : 32 * q + 4, :].bitcast(I32),
                    in_=dram_scales[0, 4 * q : 4 * q + 4, :].bitcast(I32),
                )

        rows = const.tile([P, RANK + RANK + KV], BF16)
        ones = const.tile([P, P], BF16)
        eps = const.tile([P, 1], F32)
        nc.vector.memset(ones[:], 1.0)
        nc.vector.memset(eps[:], EPS)
        nc.vector.memset(wa_plane.bitcast(I32), 0)
        nc.vector.memset(rows[:, 0 : 2 * RANK], 0.0)
        nc.vector.memset(wb_plane.bitcast(I32), 0)
        nc.vector.memset(rows[:, 2 * RANK :], 0.0)
        warm = const.tile([P, 1], F32)
        nc.scalar.activation(out=warm[:], in_=eps[:], func=ACT.Abs_reciprocal_sqrt)

        nc.sync.dma_start(out=x_all[:, 0], in_=x_pairs[0])
        load_weight(wa_words, wa_plane, wkv_a_w_words, wkv_a_w_scales)
        nc.sync.dma_start(out=rows[0:1, 0:RANK], in_=wkv_a_b.unsqueeze(0))
        nc.sync.dma_start(out=x_all[:, 1], in_=x_pairs[1])
        nc.sync.dma_start(out=rows[0:1, RANK : 2 * RANK], in_=kv_norm_w.unsqueeze(0))
        nc.sync.dma_start(out=x_all[:, 2], in_=x_pairs[2])
        load_weight(wb_words, wb_plane, wkv_b_w_words, wkv_b_w_scales)
        nc.sync.dma_start(out=rows[0:1, 2 * RANK :], in_=wkv_b_b.unsqueeze(0))
        for u in range(3, LOADS):
            nc.sync.dma_start(out=x_all[:, u], in_=x_pairs[u])

        ident_f32 = const.tile([P, P], F32)
        make_identity(nc, ident_f32[:])

        b1_all = const.tile([P, 2, P, 2], F32)
        gain_all = const.tile([P, 2, P, 2], F32)
        b2_all = const.tile([P, KV], F32)

        def spread(b):
            bank = psum.tile([P, BANK], F32, name="kv_bank", bufs=4)
            nc.tensor.matmul(
                out=bank[:], lhsT=ones[:], rhs=rows[:, b * BANK : (b + 1) * BANK], start=True, stop=True
            )
            return bank

        idle_ps = psum.tile([P, BANK], F32, name="kv_bank", bufs=4)
        for unused in range(WARM_UP):
            nc.tensor.matmul(out=idle_ps[:, 0:P], lhsT=ones[:], rhs=ones[:], start=True, stop=True)

        flipped, grouped, x_mx, kvc_mx = {}, {}, {}, {}
        latent_ps, latent, gained, sum_sq, inv_rms, kvc, kv_ps = {}, {}, {}, {}, {}, {}, {}

        def live(j):
            return 0 <= j < TILES

        def halves(n):
            return (0 if live(n + AHEAD) else 1), (2 if live(n - BEHIND) else 1)

        def flip(n):
            lo, hi = halves(n)
            if lo >= hi:
                return
            bank = psum.tile([P, 2, 2, P], F32, name="flipped")
            if live(n + AHEAD):
                j = n + AHEAD
                words = x_all[:, j // PAIR, j % PAIR, :].bitcast(F32)
                for h in range(2):
                    nc.tensor.transpose(bank[:, 0, h, :], words[:, h : DIM // 2 : 2], ident_f32[:])
            if live(n - BEHIND):
                words = kvc[n - BEHIND][:].rearrange("p h m e -> p (h m e)").bitcast(F32)
                for h in range(2):
                    nc.tensor.transpose(bank[:, 1, h, :], words[:, h * P : (h + 1) * P], ident_f32[:])
            flipped[n] = bank

        def copy_out(n):
            lo, hi = halves(n)
            if lo >= hi:
                return
            tile = work.tile([P, 2, P, PACK], BF16, align_bytes=64, name="grouped")
            nc.scalar.copy(
                out=tile[:, lo:hi].bitcast(F32), in_=flipped[n][:, lo:hi].rearrange("p s h r -> p s r h")
            )
            grouped[n] = tile

        def quantise(n):
            lo, hi = halves(n - 1)
            if lo >= hi:
                return
            codes = work.tile([P, 2 * P], U32, align_bytes=64, name="codes", bufs=6)
            plane = work.tile([P, 2 * P], U8, align_bytes=64, name="plane", bufs=6)
            cols = slice(lo * P, hi * P)
            nc.vector.quantize_mx(
                out=codes[:, cols].bitcast(FP8X4),
                scales=plane[:, cols],
                in_=grouped[n - 1][:, lo:hi].rearrange("p s r t -> p (s r t)"),
            )
            x_mx[n - 1 + AHEAD] = (codes, plane, slice(0, P))
            kvc_mx[n - 1 - BEHIND] = (codes, plane, slice(P, 2 * P))

        def multiply(out, mx, words, plane):
            codes, scales, tok = mx
            nc.tensor.matmul_mx(
                out=out,
                lhsT=codes[:, tok].bitcast(FP8X4),
                lhsT_scale=scales[:, tok],
                rhs=words.bitcast(FP8X4),
                rhs_scale=plane,
                start=True,
                stop=True,
            )

        def latent_matmul(j):
            if not live(j):
                return
            c_ps = psum.tile([P, RANK], F32, name="c_ps")
            multiply(c_ps[:], x_mx[j], wa_words[:], wa_plane)
            latent_ps[j] = c_ps

        def latent_bias(j):
            if not live(j):
                return
            c_sb = work.tile([P, 2, P, 2], F32, name="c_sb", bufs=6)
            nc.vector.tensor_tensor(
                out=c_sb[:],
                in0=latent_ps[j][:].rearrange("p (m h e) -> p h m e", h=2, e=2),
                in1=b1_all[:],
                op=ADD,
            )
            latent[j] = c_sb

        def gain(j):
            if not live(j):
                return
            c_gain = work.tile([P, 2, P, 2], F32, name="c_gain", bufs=6)
            engine = nc.vector if j < FILL else nc.gpsimd
            engine.tensor_tensor(out=c_gain[:], in0=latent[j][:], in1=gain_all[:], op=MULT)
            gained[j] = c_gain

        def sum_squares(j):
            if not live(j):
                return
            total = work.tile([P, 1], F32, name="sum_sq")
            squares = work.tile([P, 2, P, 2], BF16, name="squares", bufs=4)
            nc.scalar.activation(out=squares[:], in_=latent[j][:], func=ACT.Square, accum_out=total[:])
            sum_sq[j] = total

        def inverse_rms(j):
            if not live(j):
                return
            inverse = work.tile([P, 1], F32, name="inv_rms")
            nc.scalar.activation(
                out=inverse[:], in_=sum_sq[j][:], func=ACT.Abs_reciprocal_sqrt, bias=eps[:], scale=1.0 / RANK
            )
            inv_rms[j] = inverse

        def normalise(j):
            if not live(j):
                return
            tile = work.tile([P, 2, P, 2], BF16, name="kvc")
            nc.scalar.activation(out=tile[:], in_=gained[j][:], func=ACT.Copy, scale=inv_rms[j][:])
            kvc[j] = tile

        def project_matmul(j):
            if not live(j):
                return
            kv_ps[j] = []
            for b in range(KV // BANK):
                cols = slice(b * BANK, (b + 1) * BANK)
                bank = psum.tile([P, BANK], F32, name="kv_bank", bufs=4)
                multiply(bank[:], kvc_mx[j], wb_words[:, cols], wb_plane[:, cols])
                kv_ps[j].append(bank)

        def project_bias_and_store(j):
            if not live(j):
                return
            result = work.tile([P, 2, HEADS, HEAD_DIM], F32, name="result", bufs=32)
            for b in reversed(range(KV // BANK)):
                cols = slice(b * BANK, (b + 1) * BANK)
                nc.vector.tensor_tensor(
                    out=result[:, :, 2 * b : 2 * b + 2, :].rearrange("p w h d -> p h w d"),
                    in0=kv_ps[j][b][:].rearrange("p (h w d) -> p h w d", h=2, w=2),
                    in1=b2_all[:, cols].rearrange("p (h w d) -> p h w d", h=2, w=2),
                    op=ADD,
                )
            for w in range(2):
                nc.sync.dma_start(
                    out=out_pairs[w][j // PAIR][:, j % PAIR, :], in_=result[:, w].rearrange("p h d -> p (h d)")
                )

        for n in range(-AHEAD, TILES + BEHIND + 2):
            flip(n)
            latent_matmul(n + 1)
            if n == 1 - AHEAD:
                b1_ps = spread(0)
            latent_bias(n)
            quantise(n)
            if n == 1 - AHEAD:
                nc.vector.tensor_copy(out=b1_all[:], in_=b1_ps[:].rearrange("p (m h e) -> p h m e", h=2, e=2))
            gain(n)
            project_matmul(n - 1 - BEHIND)
            if n == 2 - AHEAD:
                gain_ps = spread(1)
            sum_squares(n - 1)
            copy_out(n)
            inverse_rms(n - 1)
            if n == 2 - AHEAD:
                nc.scalar.copy(out=gain_all[:], in_=gain_ps[:].rearrange("p (m h e) -> p h m e", h=2, e=2))
            normalise(n - 2)
            project_bias_and_store(n - 2 - BEHIND)
            if n in (2, 3):
                b2_ps = spread(n)
                nc.vector.tensor_copy(out=b2_all[:, (n - 2) * BANK : (n - 1) * BANK], in_=b2_ps[:])
